import numpy as np
import ml_dtypes


def mxq(x, axis, fmt="e4m3"):
    dtype, down = {"e4m3": (ml_dtypes.float8_e4m3fn, 7), "e5m2": (ml_dtypes.float8_e5m2, 14)}[fmt]
    v = np.moveaxis(np.asarray(x, np.float32).astype(ml_dtypes.bfloat16).astype(np.float64), axis, -1)
    blocks = v.reshape(v.shape[:-1] + (-1, 32))
    amax = np.abs(blocks).max(-1, keepdims=True)
    byte = np.maximum(np.where(amax > 0, np.frexp(amax)[1] - 1 + 127, 0) - down, 1)
    scale = np.exp2(byte - 127.0)
    codes = (blocks / scale).astype(np.float32).astype(dtype).astype(np.float64)
    return np.moveaxis((codes * scale).reshape(v.shape), -1, axis)


WIDE = False


def mx_kscale(k):
    if not WIDE:
        return np.ones(k)
    levels = np.array([10, -10, 5, -5, 0])
    a = np.random.permutation(np.resize(levels, k // 512 * 4)).reshape(k // 512, 4)
    idx = np.arange(k)
    return np.exp2(a[idx // 512, idx % 128 // 32])


BF16 = ml_dtypes.bfloat16


def bf(x):
    return np.asarray(x, np.float32).astype(BF16)


def f64(x):
    return np.asarray(x).astype(np.float64)


E2M1 = np.array([0.0, 0.5, 1.0, 1.5, 2.0, 3.0, 4.0, 6.0, -0.0, -0.5, -1.0, -1.5, -2.0, -3.0, -4.0, -6.0])


def pack_weight(w, fmt):
    k, n = w.shape
    w = f64(bf(w)).reshape(k // 32, 32, n)
    amax = np.abs(w).max(1)
    if fmt == "e4m3":
        byte = np.frexp(amax)[1] - 1 + 127 - 7
    else:
        mant, ex = np.frexp(amax / 6.0)
        byte = np.where(mant > 0.5, ex, ex - 1) + 127
    byte = np.clip(np.where(amax > 0, byte, 1), 1, 254)
    scaled = (w * np.exp2(127.0 - byte)[:, None, :]).reshape(k, n).astype(np.float32)
    by_word = np.ascontiguousarray(scaled.reshape(k // 512, 128, 4, n).transpose(0, 1, 3, 2))
    if fmt == "e4m3":
        words = by_word.astype(ml_dtypes.float8_e4m3fn).view(np.uint8)
    else:
        c = by_word.astype(ml_dtypes.float4_e2m1fn).view(np.uint8) & 0xF
        words = c[..., 0::2] | (c[..., 1::2] << 4)
    return np.ascontiguousarray(words), np.ascontiguousarray(byte.astype(np.uint8).reshape(k // 512, 16, n))


def unpack_weight(words, scales, fmt):
    g, p, n, _ = words.shape
    if fmt == "e4m3":
        vals = np.ascontiguousarray(words).view(ml_dtypes.float8_e4m3fn).astype(np.float64)
    else:
        nib = np.empty((g, p, n, 4), np.uint8)
        nib[..., 0::2] = words & 0xF
        nib[..., 1::2] = words >> 4
        vals = E2M1[nib]
    vals = vals * np.repeat(np.exp2(scales.astype(np.float64) - 127.0), 8, axis=1)[..., None]
    return vals.transpose(0, 1, 3, 2).reshape(g * 512, n)

def pack4(w):
    words, scales = pack_weight(w, "e2m1")
    return words.reshape(words.shape[0], 128, -1), scales


def unpack4(words, scales):
    return unpack_weight(words.reshape(words.shape[0], 128, -1, 2), scales, "e2m1")


B, N, C, H, F = 2, 512, 1024, 8, 2752
D = C // H


def setup_inputs():
    a = mx_kscale(C)[:D]
    t = np.tile(a, H)
    z = np.random.standard_normal((B, H, D, D)) * np.sqrt((N + N * N / C) / D)
    e = np.exp(z - z.max(-1, keepdims=True))
    attn = bf(e / e.sum(-1, keepdims=True) * a[:, None])
    v = bf(np.random.standard_normal((B, H, N, D)))
    words, scales = pack4((np.random.standard_normal((C, C)) / np.sqrt(C) / t).T)
    return {"attn": attn,
            "v": v,
            "w_proj_words": words,
            "w_proj_scales": scales,
            "b_proj": bf(0.1 * np.random.standard_normal(C)),
            "shortcut": bf(np.random.standard_normal((B, N, C)))}


def reference(attn, v, w_proj_words, w_proj_scales, b_proj, shortcut):
    o = f64(attn) @ f64(v).transpose(0, 1, 3, 2)
    o = o.transpose(0, 1, 3, 2).reshape(B, N, C)
    return (mxq(o, 2, "e4m3") @ unpack4(w_proj_words, w_proj_scales)) + f64(b_proj) + f64(shortcut)

@@ -1,0 +1,185 @@
+from contextlib import ExitStack
+
+import concourse.mybir as mybir
+from concourse.masks import make_identity
+
+BF16 = mybir.dt.bfloat16
+F32 = mybir.dt.float32
+I32 = mybir.dt.int32
+U8 = mybir.dt.uint8
+U32 = mybir.dt.uint32
+FP8X4 = mybir.dt.float8_e4m3fn_x4
+FP4X4 = mybir.dt.float4_e2m1fn_x4
+ADD = mybir.AluOpType.add
+
+P = 128
+WIDTH = 1024
+ROW_TILES = 8
+BATCHES = 2
+SLABS = 8
+PASSES = 2
+SLABS_PER_PASS = 4
+HEADS_PER_TILE = 2
+HEAD_ROWS = 64
+HEADS = 8
+HALF = 512
+HALVES = 2
+PAIRS = 2
+
+MX_LAG = 4
+
+FLOPS = 2 * 1024 * 1024 * 1024 + 2 * 16 * 128 * 128 * 512
+
+
+def tile_transposedattentiontransformer_pb_kernel(
+    tc, attn, v, w_proj_words, w_proj_scales, b_proj, shortcut, out
+):
+    nc = tc.nc
+    v_rows = v.rearrange("b g (r s) e -> (b g r) (s e)", s=SLABS)
+    attn_rows = attn.rearrange("b g (a x) e -> b (g a) (x e)", x=SLABS)
+    shortcut_rows = shortcut.flatten_outer_dims()
+    out_rows = out.flatten_outer_dims()
+
+    with ExitStack() as ctx:
+        keep = ctx.enter_context(tc.tile_pool(name="keep", bufs=1))
+        banks = ctx.enter_context(tc.psum_pool(name="banks", bufs=8))
+        ctx.enter_context(tc.manual_schedule())
+
+        ident_bf16 = keep.tile([P, P], BF16)
+        ident_f32 = keep.tile([P, P], F32)
+        ones = keep.tile([P, P], BF16)
+        bias_row = keep.tile([P, WIDTH], BF16)
+        bias_all = keep.tile([P, WIDTH], BF16)
+        attn_sb = keep.tile([P, BATCHES, WIDTH], BF16)
+        attn_t = keep.tile([P, BATCHES, WIDTH], BF16)
+        v_sb = keep.tile([P, ROW_TILES, WIDTH], BF16)
+        v_t = keep.tile([P, ROW_TILES, WIDTH], BF16)
+        y_sb = keep.tile([P, ROW_TILES * HEADS_PER_TILE, HALF], BF16)
+        y_grouped = keep.tile([P, ROW_TILES, WIDTH], BF16, align_bytes=64)
+        y_codes = keep.tile([P, ROW_TILES, PASSES * P], U32, align_bytes=64)
+        y_scales = keep.tile([P, ROW_TILES, PASSES * P], U8, align_bytes=64)
+        w_words = keep.tile([P, PASSES, 2 * WIDTH], U8, align_bytes=64)
+        w_scales = keep.tile([P, PASSES, WIDTH], U8, align_bytes=64)
+        shortcut_sb = keep.tile([P, ROW_TILES, WIDTH], BF16)
+        result = keep.tile([P, ROW_TILES, WIDTH], F32)
+
+        make_identity(nc, ident_bf16[:])
+        make_identity(nc, ident_f32[:])
+        nc.vector.memset(bias_row[:], 0.0)
+        nc.vector.memset(ones[:], 1.0)
+        nc.vector.memset(w_scales[:].bitcast(I32), 0)
+
+        for b in range(BATCHES):
+            nc.sync.dma_start(out=attn_sb[:, b, :], in_=attn_rows[b])
+        nc.sync.dma_start(out=bias_row[0:1, :], in_=b_proj.unsqueeze(0))
+        for rt in range(ROW_TILES):
+            rows = slice(rt * P, (rt + 1) * P)
+            nc.sync.dma_start(out=v_sb[:, rt, :], in_=v_rows[rows, :])
+            nc.sync.dma_start(out=shortcut_sb[:, rt, :], in_=shortcut_rows[rows, :])
+        for quadrant in range(4):
+            nc.sync.dma_start(
+                out=w_scales[32 * quadrant : 32 * quadrant + 4, :, :].bitcast(I32),
+                in_=w_proj_scales.bitcast(I32)[:, 4 * quadrant : 4 * quadrant + 4, :].rearrange("c i n -> i c n"),
+            )
+        nc.sync.dma_start(
+            out=w_words[:].bitcast(I32), in_=w_proj_words.bitcast(I32).rearrange("c p n -> p c n")
+        )
+
+        def flip_attn(b):
+            bank = banks.tile([P, SLABS, P], BF16, tag="bank")
+            for x in range(SLABS):
+                nc.tensor.transpose(bank[:, x, :], attn_sb[:, b, x * P : (x + 1) * P], ident_bf16[:])
+            nc.scalar.copy(
+                out=attn_t[:, b, :].rearrange("e (a x) -> e a x", x=SLABS),
+                in_=bank[:].rearrange("e x a -> e a x"),
+            )
+
+        def flip_v(rt):
+            bank = banks.tile([P, HEADS_PER_TILE, SLABS_PER_PASS, PASSES, HEAD_ROWS], BF16, tag="bank")
+            for slab in range(SLABS):
+                c, j = divmod(slab, SLABS_PER_PASS)
+                nc.tensor.transpose(bank[:, :, j, c, :], v_sb[:, rt, slab * P : (slab + 1) * P], ident_bf16[:])
+            nc.scalar.copy(out=v_t[:, rt, :], in_=bank[:].rearrange("e h j c r -> e (h j c r)"))
+
+        def attend(rt):
+            for h in range(HEADS_PER_TILE):
+                head = rt * HEADS_PER_TILE + h
+                b, g = divmod(head, HEADS)
+                bank = banks.tile([P, HALF], F32, tag="bank")
+                for j in range(SLABS_PER_PASS):
+                    first = (h * SLABS_PER_PASS + j) * P
+                    nc.tensor.matmul(
+                        out=bank[:, j * P : (j + 1) * P],
+                        lhsT=v_t[:, rt, first : first + P],
+                        rhs=attn_t[:, b, g * P : (g + 1) * P],
+                        start=True,
+                        stop=True,
+                    )
+                copy_out = nc.vector.tensor_copy if h == 0 else nc.scalar.copy
+                copy_out(
+                    out=y_sb[:, head, :].rearrange("m (u p e) -> m u p e", u=PAIRS, e=2),
+                    in_=bank[:].rearrange("m (p u e) -> m u p e", u=PAIRS, e=2),
+                )
+
+        def flip_y(rt):
+            bank = banks.tile([P, PAIRS, PASSES, HEADS_PER_TILE, HEAD_ROWS], F32, tag="bank")
+            for h in range(HEADS_PER_TILE):
+                head = rt * HEADS_PER_TILE + h
+                for u in range(PAIRS):
+                    nc.tensor.transpose(
+                        bank[:, u, :, h, :],
+                        y_sb[:, head, u * 2 * P : (u + 1) * 2 * P].bitcast(F32),
+                        ident_f32[:],
+                    )
+            nc.scalar.copy(
+                out=y_grouped[:, rt, :].bitcast(F32).rearrange("p (s u) -> p s u", u=PAIRS),
+                in_=bank[:].rearrange("p u c h r -> p (c h r) u"),
+            )
+
+        def quantise(rt):
+            nc.vector.quantize_mx(
+                out=y_codes[:, rt, :].bitcast(FP8X4), scales=y_scales[:, rt, :], in_=y_grouped[:, rt, :]
+            )
+
+        def project(rt):
+            for half in range(HALVES):
+                cols = slice(half * HALF, (half + 1) * HALF)
+                bank = banks.tile([P, HALF], F32, tag="bank")
+                for c in range(PASSES):
+                    nc.tensor.matmul_mx(
+                        out=bank[:],
+                        lhsT=y_codes[:, rt, c * P : (c + 1) * P].bitcast(FP8X4),
+                        lhsT_scale=y_scales[:, rt, c * P : (c + 1) * P],
+                        rhs=w_words[:, c, 2 * half * HALF : 2 * (half + 1) * HALF].bitcast(FP4X4),
+                        rhs_scale=w_scales[:, c, cols],
+                        start=(c == 0),
+                        stop=(c == PASSES - 1),
+                    )
+                nc.vector.tensor_tensor(out=result[:, rt, cols], in0=bank[:], in1=result[:, rt, cols], op=ADD)
+                nc.sync.dma_start(out=out_rows[rt * P : (rt + 1) * P, cols], in_=result[:, rt, cols])
+
+        for b in range(BATCHES):
+            flip_attn(b)
+        for half in range(HALVES):
+            cols = slice(half * HALF, (half + 1) * HALF)
+            bank = banks.tile([P, HALF], F32, tag="bank")
+            nc.tensor.matmul(out=bank[:], lhsT=ones[:], rhs=bias_row[:, cols], start=True, stop=True)
+            nc.vector.tensor_copy(out=bias_all[:, cols], in_=bank[:])
+
+        for rt in range(ROW_TILES):
+            nc.gpsimd.tensor_tensor(out=result[:, rt, :], in0=shortcut_sb[:, rt, :], in1=bias_all[:], op=ADD)
+
+        def is_tile(rt):
+            return 0 <= rt < ROW_TILES
+
+        for step in range(ROW_TILES + MX_LAG):
+            if is_tile(step):
+                flip_v(step)
+            if is_tile(step - 1):
+                attend(step - 1)
+            if is_tile(step - 2):
+                flip_y(step - 2)
+            if is_tile(step - 3):
+                quantise(step - 3)
+            if is_tile(step - MX_LAG):
+                project(step - MX_LAG)

@@ -26,7 +26,7 @@ HALF = 512
 HALVES = 2
 PAIRS = 2
 
-MX_LAG = 4
+MX_LAG = 10
 
 FLOPS = 2 * 1024 * 1024 * 1024 + 2 * 16 * 128 * 128 * 512
 
@@ -131,7 +131,7 @@ def tile_transposedattentiontransformer_pb_kernel(
                         y_sb[:, head, u * 2 * P : (u + 1) * 2 * P].bitcast(F32),
                         ident_f32[:],
                     )
-            nc.scalar.copy(
+            nc.vector.tensor_copy(
                 out=y_grouped[:, rt, :].bitcast(F32).rearrange("p (s u) -> p s u", u=PAIRS),
                 in_=bank[:].rearrange("p u c h r -> p (c h r) u"),
             )

@@ -26,7 +26,7 @@ HALF = 512
 HALVES = 2
 PAIRS = 2
 
-MX_LAG = 10
+MX_LAG = 4
 
 FLOPS = 2 * 1024 * 1024 * 1024 + 2 * 16 * 128 * 128 * 512
 
@@ -65,13 +65,13 @@ def tile_transposedattentiontransformer_pb_kernel(
 
         make_identity(nc, ident_bf16[:])
         make_identity(nc, ident_f32[:])
-        nc.vector.memset(bias_row[:], 0.0)
+        nc.vector.memset(bias_row[:].bitcast(I32), 0)
         nc.vector.memset(ones[:], 1.0)
         nc.vector.memset(w_scales[:].bitcast(I32), 0)
 
+        nc.scalar.dma_start(out=bias_row[0:1, :], in_=b_proj.unsqueeze(0))
         for b in range(BATCHES):
             nc.sync.dma_start(out=attn_sb[:, b, :], in_=attn_rows[b])
-        nc.sync.dma_start(out=bias_row[0:1, :], in_=b_proj.unsqueeze(0))
         for rt in range(ROW_TILES):
             rows = slice(rt * P, (rt + 1) * P)
             nc.sync.dma_start(out=v_sb[:, rt, :], in_=v_rows[rows, :])
@@ -131,7 +131,7 @@ def tile_transposedattentiontransformer_pb_kernel(
                         y_sb[:, head, u * 2 * P : (u + 1) * 2 * P].bitcast(F32),
                         ident_f32[:],
                     )
-            nc.vector.tensor_copy(
+            nc.scalar.copy(
                 out=y_grouped[:, rt, :].bitcast(F32).rearrange("p (s u) -> p s u", u=PAIRS),
                 in_=bank[:].rearrange("p u c h r -> p (c h r) u"),
             )
@@ -158,16 +158,20 @@ def tile_transposedattentiontransformer_pb_kernel(
                 nc.vector.tensor_tensor(out=result[:, rt, cols], in0=bank[:], in1=result[:, rt, cols], op=ADD)
                 nc.sync.dma_start(out=out_rows[rt * P : (rt + 1) * P, cols], in_=result[:, rt, cols])
 
-        for b in range(BATCHES):
-            flip_attn(b)
+        flip_attn(0)
         for half in range(HALVES):
             cols = slice(half * HALF, (half + 1) * HALF)
             bank = banks.tile([P, HALF], F32, tag="bank")
             nc.tensor.matmul(out=bank[:], lhsT=ones[:], rhs=bias_row[:, cols], start=True, stop=True)
             nc.vector.tensor_copy(out=bias_all[:, cols], in_=bank[:])
+        flip_attn(1)
 
         for rt in range(ROW_TILES):
-            nc.gpsimd.tensor_tensor(out=result[:, rt, :], in0=shortcut_sb[:, rt, :], in1=bias_all[:], op=ADD)
+            for half in range(HALVES):
+                cols = slice(half * HALF, (half + 1) * HALF)
+                nc.gpsimd.tensor_tensor(
+                    out=result[:, rt, cols], in0=shortcut_sb[:, rt, cols], in1=bias_all[:, cols], op=ADD
+                )
 
         def is_tile(rt):
             return 0 <= rt < ROW_TILES
@@ -175,10 +179,10 @@ def tile_transposedattentiontransformer_pb_kernel(
         for step in range(ROW_TILES + MX_LAG):
             if is_tile(step):
                 flip_v(step)
-            if is_tile(step - 1):
-                attend(step - 1)
             if is_tile(step - 2):
                 flip_y(step - 2)
+            if is_tile(step - 1):
+                attend(step - 1)
             if is_tile(step - 3):
                 quantise(step - 3)
             if is_tile(step - MX_LAG):

@@ -25,6 +25,7 @@ HEADS = 8
 HALF = 512
 HALVES = 2
 PAIRS = 2
+VECTOR_SUMS = 2
 
 MX_LAG = 4
 
@@ -47,14 +48,13 @@ def tile_transposedattentiontransformer_pb_kernel(
 
         ident_bf16 = keep.tile([P, P], BF16)
         ident_f32 = keep.tile([P, P], F32)
-        ones = keep.tile([P, P], BF16)
-        bias_row = keep.tile([P, WIDTH], BF16)
+        bias_slabs = keep.tile([P, P], BF16)
         bias_all = keep.tile([P, WIDTH], BF16)
         attn_sb = keep.tile([P, BATCHES, WIDTH], BF16)
         attn_t = keep.tile([P, BATCHES, WIDTH], BF16)
         v_sb = keep.tile([P, ROW_TILES, WIDTH], BF16)
         v_t = keep.tile([P, ROW_TILES, WIDTH], BF16)
-        y_sb = keep.tile([P, ROW_TILES * HEADS_PER_TILE, HALF], BF16)
+        y_sb = keep.tile([P, ROW_TILES, WIDTH], BF16)
         y_grouped = keep.tile([P, ROW_TILES, WIDTH], BF16, align_bytes=64)
         y_codes = keep.tile([P, ROW_TILES, PASSES * P], U32, align_bytes=64)
         y_scales = keep.tile([P, ROW_TILES, PASSES * P], U8, align_bytes=64)
@@ -63,13 +63,12 @@ def tile_transposedattentiontransformer_pb_kernel(
         shortcut_sb = keep.tile([P, ROW_TILES, WIDTH], BF16)
         result = keep.tile([P, ROW_TILES, WIDTH], F32)
 
+        nc.gpsimd.memset(bias_slabs[:], 0.0)
         make_identity(nc, ident_bf16[:])
         make_identity(nc, ident_f32[:])
-        nc.vector.memset(bias_row[:].bitcast(I32), 0)
-        nc.vector.memset(ones[:], 1.0)
         nc.vector.memset(w_scales[:].bitcast(I32), 0)
 
-        nc.scalar.dma_start(out=bias_row[0:1, :], in_=b_proj.unsqueeze(0))
+        nc.sync.dma_start(out=bias_slabs[0:SLABS, :], in_=b_proj.rearrange("(s n) -> s n", n=P))
         for b in range(BATCHES):
             nc.sync.dma_start(out=attn_sb[:, b, :], in_=attn_rows[b])
         for rt in range(ROW_TILES):
@@ -102,34 +101,33 @@ def tile_transposedattentiontransformer_pb_kernel(
             nc.scalar.copy(out=v_t[:, rt, :], in_=bank[:].rearrange("e h j c r -> e (h j c r)"))
 
         def attend(rt):
+            bank = banks.tile([P, HEADS_PER_TILE, HALF], BF16, tag="bank")
             for h in range(HEADS_PER_TILE):
-                head = rt * HEADS_PER_TILE + h
-                b, g = divmod(head, HEADS)
-                bank = banks.tile([P, HALF], F32, tag="bank")
+                b, g = divmod(rt * HEADS_PER_TILE + h, HEADS)
                 for j in range(SLABS_PER_PASS):
                     first = (h * SLABS_PER_PASS + j) * P
                     nc.tensor.matmul(
-                        out=bank[:, j * P : (j + 1) * P],
+                        out=bank[:, h, j * P : (j + 1) * P],
                         lhsT=v_t[:, rt, first : first + P],
                         rhs=attn_t[:, b, g * P : (g + 1) * P],
                         start=True,
                         stop=True,
                     )
-                copy_out = nc.vector.tensor_copy if h == 0 else nc.scalar.copy
-                copy_out(
-                    out=y_sb[:, head, :].rearrange("m (u p e) -> m u p e", u=PAIRS, e=2),
-                    in_=bank[:].rearrange("m (p u e) -> m u p e", u=PAIRS, e=2),
-                )
+            nc.scalar.copy(
+                out=y_sb[:, rt, :].bitcast(F32).rearrange("m (h u p) -> m h u p", h=HEADS_PER_TILE, u=PAIRS),
+                in_=bank[:]
+                .rearrange("m h k -> m (h k)")
+                .bitcast(F32)
+                .rearrange("m (h p u) -> m h u p", h=HEADS_PER_TILE, u=PAIRS),
+            )
 
         def flip_y(rt):
             bank = banks.tile([P, PAIRS, PASSES, HEADS_PER_TILE, HEAD_ROWS], F32, tag="bank")
             for h in range(HEADS_PER_TILE):
-                head = rt * HEADS_PER_TILE + h
                 for u in range(PAIRS):
+                    first = (h * PAIRS + u) * 2 * P
                     nc.tensor.transpose(
-                        bank[:, u, :, h, :],
-                        y_sb[:, head, u * 2 * P : (u + 1) * 2 * P].bitcast(F32),
-                        ident_f32[:],
+                        bank[:, u, :, h, :], y_sb[:, rt, first : first + 2 * P].bitcast(F32), ident_f32[:]
                     )
             nc.scalar.copy(
                 out=y_grouped[:, rt, :].bitcast(F32).rearrange("p (s u) -> p s u", u=PAIRS),
@@ -160,16 +158,24 @@ def tile_transposedattentiontransformer_pb_kernel(
 
         flip_attn(0)
         for half in range(HALVES):
-            cols = slice(half * HALF, (half + 1) * HALF)
             bank = banks.tile([P, HALF], F32, tag="bank")
-            nc.tensor.matmul(out=bank[:], lhsT=ones[:], rhs=bias_row[:, cols], start=True, stop=True)
-            nc.vector.tensor_copy(out=bias_all[:, cols], in_=bank[:])
+            for j in range(SLABS_PER_PASS):
+                s = half * SLABS_PER_PASS + j
+                nc.tensor.matmul(
+                    out=bank[:, j * P : (j + 1) * P],
+                    lhsT=ident_bf16[:, s : s + 1].to_broadcast([P, P]),
+                    rhs=bias_slabs[:],
+                    start=True,
+                    stop=True,
+                )
+            nc.vector.tensor_copy(out=bias_all[:, half * HALF : (half + 1) * HALF], in_=bank[:])
         flip_attn(1)
 
         for rt in range(ROW_TILES):
+            adder = nc.vector if rt < VECTOR_SUMS else nc.gpsimd
             for half in range(HALVES):
                 cols = slice(half * HALF, (half + 1) * HALF)
-                nc.gpsimd.tensor_tensor(
+                adder.tensor_tensor(
                     out=result[:, rt, cols], in0=shortcut_sb[:, rt, cols], in1=bias_all[:, cols], op=ADD
                 )
 
@@ -179,10 +185,10 @@ def tile_transposedattentiontransformer_pb_kernel(
         for step in range(ROW_TILES + MX_LAG):
             if is_tile(step):
                 flip_v(step)
-            if is_tile(step - 2):
-                flip_y(step - 2)
             if is_tile(step - 1):
                 attend(step - 1)
+            if is_tile(step - 2):
+                flip_y(step - 2)
             if is_tile(step - 3):
                 quantise(step - 3)
             if is_tile(step - MX_LAG):

@@ -25,7 +25,6 @@ HEADS = 8
 HALF = 512
 HALVES = 2
 PAIRS = 2
-VECTOR_SUMS = 2
 
 MX_LAG = 4
 
@@ -71,18 +70,28 @@ def tile_transposedattentiontransformer_pb_kernel(
         nc.sync.dma_start(out=bias_slabs[0:SLABS, :], in_=b_proj.rearrange("(s n) -> s n", n=P))
         for b in range(BATCHES):
             nc.sync.dma_start(out=attn_sb[:, b, :], in_=attn_rows[b])
-        for rt in range(ROW_TILES):
-            rows = slice(rt * P, (rt + 1) * P)
-            nc.sync.dma_start(out=v_sb[:, rt, :], in_=v_rows[rows, :])
-            nc.sync.dma_start(out=shortcut_sb[:, rt, :], in_=shortcut_rows[rows, :])
+
+        def load_v(rt):
+            nc.sync.dma_start(out=v_sb[:, rt, :], in_=v_rows[rt * P : (rt + 1) * P, :])
+
+        def load_shortcut(rt):
+            nc.sync.dma_start(out=shortcut_sb[:, rt, :], in_=shortcut_rows[rt * P : (rt + 1) * P, :])
+
+        for rt in range(MX_LAG):
+            load_v(rt)
+        nc.sync.dma_start(
+            out=w_words[:].bitcast(I32), in_=w_proj_words.bitcast(I32).rearrange("c p n -> p c n")
+        )
         for quadrant in range(4):
             nc.sync.dma_start(
                 out=w_scales[32 * quadrant : 32 * quadrant + 4, :, :].bitcast(I32),
                 in_=w_proj_scales.bitcast(I32)[:, 4 * quadrant : 4 * quadrant + 4, :].rearrange("c i n -> i c n"),
             )
-        nc.sync.dma_start(
-            out=w_words[:].bitcast(I32), in_=w_proj_words.bitcast(I32).rearrange("c p n -> p c n")
-        )
+        for rt in range(MX_LAG, ROW_TILES):
+            load_shortcut(rt - MX_LAG)
+            load_v(rt)
+        for rt in range(ROW_TILES - MX_LAG, ROW_TILES):
+            load_shortcut(rt)
 
         def flip_attn(b):
             bank = banks.tile([P, SLABS, P], BF16, tag="bank")
@@ -172,10 +181,9 @@ def tile_transposedattentiontransformer_pb_kernel(
         flip_attn(1)
 
         for rt in range(ROW_TILES):
-            adder = nc.vector if rt < VECTOR_SUMS else nc.gpsimd
             for half in range(HALVES):
                 cols = slice(half * HALF, (half + 1) * HALF)
-                adder.tensor_tensor(
+                nc.gpsimd.tensor_tensor(
                     out=result[:, rt, cols], in0=shortcut_sb[:, rt, cols], in1=bias_all[:, cols], op=ADD
                 )
 

@@ -97,7 +97,7 @@ def tile_transposedattentiontransformer_pb_kernel(
             bank = banks.tile([P, SLABS, P], BF16, tag="bank")
             for x in range(SLABS):
                 nc.tensor.transpose(bank[:, x, :], attn_sb[:, b, x * P : (x + 1) * P], ident_bf16[:])
-            nc.scalar.copy(
+            nc.vector.tensor_copy(
                 out=attn_t[:, b, :].rearrange("e (a x) -> e a x", x=SLABS),
                 in_=bank[:].rearrange("e x a -> e a x"),
             )
@@ -165,7 +165,6 @@ def tile_transposedattentiontransformer_pb_kernel(
                 nc.vector.tensor_tensor(out=result[:, rt, cols], in0=bank[:], in1=result[:, rt, cols], op=ADD)
                 nc.sync.dma_start(out=out_rows[rt * P : (rt + 1) * P, cols], in_=result[:, rt, cols])
 
-        flip_attn(0)
         for half in range(HALVES):
             bank = banks.tile([P, HALF], F32, tag="bank")
             for j in range(SLABS_PER_PASS):
@@ -178,7 +177,8 @@ def tile_transposedattentiontransformer_pb_kernel(
                     stop=True,
                 )
             nc.vector.tensor_copy(out=bias_all[:, half * HALF : (half + 1) * HALF], in_=bank[:])
-        flip_attn(1)
+        for b in range(BATCHES):
+            flip_attn(b)
 
         for rt in range(ROW_TILES):
             for half in range(HALVES):

@@ -27,6 +27,8 @@ HALVES = 2
 PAIRS = 2
 
 MX_LAG = 4
+EARLY_SHORTCUTS = 2
+SHORTCUT_BEHIND = MX_LAG + 1 - EARLY_SHORTCUTS
 
 FLOPS = 2 * 1024 * 1024 * 1024 + 2 * 16 * 128 * 128 * 512
 
@@ -77,8 +79,10 @@ def tile_transposedattentiontransformer_pb_kernel(
         def load_shortcut(rt):
             nc.sync.dma_start(out=shortcut_sb[:, rt, :], in_=shortcut_rows[rt * P : (rt + 1) * P, :])
 
-        for rt in range(MX_LAG):
+        for rt in range(MX_LAG + 1):
             load_v(rt)
+            if rt < EARLY_SHORTCUTS:
+                load_shortcut(rt)
         nc.sync.dma_start(
             out=w_words[:].bitcast(I32), in_=w_proj_words.bitcast(I32).rearrange("c p n -> p c n")
         )
@@ -87,10 +91,10 @@ def tile_transposedattentiontransformer_pb_kernel(
                 out=w_scales[32 * quadrant : 32 * quadrant + 4, :, :].bitcast(I32),
                 in_=w_proj_scales.bitcast(I32)[:, 4 * quadrant : 4 * quadrant + 4, :].rearrange("c i n -> i c n"),
             )
-        for rt in range(MX_LAG, ROW_TILES):
-            load_shortcut(rt - MX_LAG)
+        for rt in range(MX_LAG + 1, ROW_TILES):
+            load_shortcut(rt - SHORTCUT_BEHIND)
             load_v(rt)
-        for rt in range(ROW_TILES - MX_LAG, ROW_TILES):
+        for rt in range(ROW_TILES - SHORTCUT_BEHIND, ROW_TILES):
             load_shortcut(rt)
 
         def flip_attn(b):

@@ -27,7 +27,7 @@ HALVES = 2
 PAIRS = 2
 
 MX_LAG = 4
-EARLY_SHORTCUTS = 2
+EARLY_SHORTCUTS = 3
 SHORTCUT_BEHIND = MX_LAG + 1 - EARLY_SHORTCUTS
 
 FLOPS = 2 * 1024 * 1024 * 1024 + 2 * 16 * 128 * 128 * 512

@@ -26,10 +26,7 @@ HALF = 512
 HALVES = 2
 PAIRS = 2
 
-MX_LAG = 4
-EARLY_SHORTCUTS = 3
-SHORTCUT_BEHIND = MX_LAG + 1 - EARLY_SHORTCUTS
-
+MX_LAG = 3
 FLOPS = 2 * 1024 * 1024 * 1024 + 2 * 16 * 128 * 128 * 512
 
 
@@ -70,7 +67,7 @@ def tile_transposedattentiontransformer_pb_kernel(
         nc.vector.memset(w_scales[:].bitcast(I32), 0)
 
         nc.sync.dma_start(out=bias_slabs[0:SLABS, :], in_=b_proj.rearrange("(s n) -> s n", n=P))
-        for b in range(BATCHES):
+        def load_attn(b):
             nc.sync.dma_start(out=attn_sb[:, b, :], in_=attn_rows[b])
 
         def load_v(rt):
@@ -79,23 +76,27 @@ def tile_transposedattentiontransformer_pb_kernel(
         def load_shortcut(rt):
             nc.sync.dma_start(out=shortcut_sb[:, rt, :], in_=shortcut_rows[rt * P : (rt + 1) * P, :])
 
-        for rt in range(MX_LAG + 1):
-            load_v(rt)
-            if rt < EARLY_SHORTCUTS:
-                load_shortcut(rt)
-        nc.sync.dma_start(
-            out=w_words[:].bitcast(I32), in_=w_proj_words.bitcast(I32).rearrange("c p n -> p c n")
-        )
-        for quadrant in range(4):
+        def load_w():
             nc.sync.dma_start(
-                out=w_scales[32 * quadrant : 32 * quadrant + 4, :, :].bitcast(I32),
-                in_=w_proj_scales.bitcast(I32)[:, 4 * quadrant : 4 * quadrant + 4, :].rearrange("c i n -> i c n"),
+                out=w_words[:].bitcast(I32), in_=w_proj_words.bitcast(I32).rearrange("c p n -> p c n")
             )
-        for rt in range(MX_LAG + 1, ROW_TILES):
-            load_shortcut(rt - SHORTCUT_BEHIND)
+            for quadrant in range(4):
+                nc.sync.dma_start(
+                    out=w_scales[32 * quadrant : 32 * quadrant + 4, :, :].bitcast(I32),
+                    in_=w_proj_scales.bitcast(I32)[:, 4 * quadrant : 4 * quadrant + 4, :].rearrange("c i n -> i c n"),
+                )
+
+        load_attn(0)
+        for rt in range(3):
             load_v(rt)
-        for rt in range(ROW_TILES - SHORTCUT_BEHIND, ROW_TILES):
-            load_shortcut(rt)
+        load_w()
+        load_shortcut(0)
+        load_shortcut(1)
+        load_attn(1)
+        for rt in range(3, ROW_TILES):
+            load_v(rt)
+            load_shortcut(rt - 1)
+        load_shortcut(ROW_TILES - 1)
 
         def flip_attn(b):
             bank = banks.tile([P, SLABS, P], BF16, tag="bank")
@@ -111,7 +112,9 @@ def tile_transposedattentiontransformer_pb_kernel(
             for slab in range(SLABS):
                 c, j = divmod(slab, SLABS_PER_PASS)
                 nc.tensor.transpose(bank[:, :, j, c, :], v_sb[:, rt, slab * P : (slab + 1) * P], ident_bf16[:])
-            nc.scalar.copy(out=v_t[:, rt, :], in_=bank[:].rearrange("e h j c r -> e (h j c r)"))
+            nc.scalar.copy(
+                out=v_t[:, rt, :].bitcast(F32), in_=bank[:].rearrange("e h j c r -> e (h j c r)").bitcast(F32)
+            )
 
         def attend(rt):
             bank = banks.tile([P, HEADS_PER_TILE, HALF], BF16, tag="bank")
@@ -180,16 +183,11 @@ def tile_transposedattentiontransformer_pb_kernel(
                     start=True,
                     stop=True,
                 )
-            nc.vector.tensor_copy(out=bias_all[:, half * HALF : (half + 1) * HALF], in_=bank[:])
-        for b in range(BATCHES):
-            flip_attn(b)
+            nc.scalar.copy(out=bias_all[:, half * HALF : (half + 1) * HALF], in_=bank[:])
+        flip_attn(0)
 
-        for rt in range(ROW_TILES):
-            for half in range(HALVES):
-                cols = slice(half * HALF, (half + 1) * HALF)
-                nc.gpsimd.tensor_tensor(
-                    out=result[:, rt, cols], in0=shortcut_sb[:, rt, cols], in1=bias_all[:, cols], op=ADD
-                )
+        def add_bias(rt):
+            nc.vector.tensor_tensor(out=result[:, rt, :], in0=shortcut_sb[:, rt, :], in1=bias_all[:], op=ADD)
 
         def is_tile(rt):
             return 0 <= rt < ROW_TILES
@@ -197,11 +195,14 @@ def tile_transposedattentiontransformer_pb_kernel(
         for step in range(ROW_TILES + MX_LAG):
             if is_tile(step):
                 flip_v(step)
+            if is_tile(step - 2):
+                flip_y(step - 2)
+            if step == 3:
+                flip_attn(1)
             if is_tile(step - 1):
                 attend(step - 1)
             if is_tile(step - 2):
-                flip_y(step - 2)
-            if is_tile(step - 3):
-                quantise(step - 3)
+                add_bias(step - 2)
+                quantise(step - 2)
             if is_tile(step - MX_LAG):
                 project(step - MX_LAG)

@@ -26,7 +26,12 @@ HALF = 512
 HALVES = 2
 PAIRS = 2
 
-MX_LAG = 3
+PROJECT_AFTER = (5, 7, 8, 9)
+GROUPED_ON_VECTOR = (0, 2, 4)
+ADDED_ON_GPSIMD = 5
+
+WARM_UP = 4
+
 FLOPS = 2 * 1024 * 1024 * 1024 + 2 * 16 * 128 * 128 * 512
 
 
@@ -61,12 +66,13 @@ def tile_transposedattentiontransformer_pb_kernel(
         shortcut_sb = keep.tile([P, ROW_TILES, WIDTH], BF16)
         result = keep.tile([P, ROW_TILES, WIDTH], F32)
 
+        warm_sb = keep.tile([P, HALF], BF16)
+        nc.vector.memset(warm_sb[:].bitcast(F32), 0.0)
         nc.gpsimd.memset(bias_slabs[:], 0.0)
         make_identity(nc, ident_bf16[:])
         make_identity(nc, ident_f32[:])
         nc.vector.memset(w_scales[:].bitcast(I32), 0)
 
-        nc.sync.dma_start(out=bias_slabs[0:SLABS, :], in_=b_proj.rearrange("(s n) -> s n", n=P))
         def load_attn(b):
             nc.sync.dma_start(out=attn_sb[:, b, :], in_=attn_rows[b])
 
@@ -87,16 +93,18 @@ def tile_transposedattentiontransformer_pb_kernel(
                 )
 
         load_attn(0)
-        for rt in range(3):
-            load_v(rt)
-        load_w()
-        load_shortcut(0)
-        load_shortcut(1)
+        load_v(0)
+        nc.sync.dma_start(out=bias_slabs[0:SLABS, :], in_=b_proj.rearrange("(s n) -> s n", n=P))
+        load_v(1)
         load_attn(1)
+        load_v(2)
         for rt in range(3, ROW_TILES):
+            load_shortcut(rt - 3)
+            if rt == 4:
+                load_w()
             load_v(rt)
-            load_shortcut(rt - 1)
-        load_shortcut(ROW_TILES - 1)
+        for rt in range(ROW_TILES - 3, ROW_TILES):
+            load_shortcut(rt)
 
         def flip_attn(b):
             bank = banks.tile([P, SLABS, P], BF16, tag="bank")
@@ -145,10 +153,12 @@ def tile_transposedattentiontransformer_pb_kernel(
                     nc.tensor.transpose(
                         bank[:, u, :, h, :], y_sb[:, rt, first : first + 2 * P].bitcast(F32), ident_f32[:]
                     )
-            nc.scalar.copy(
-                out=y_grouped[:, rt, :].bitcast(F32).rearrange("p (s u) -> p s u", u=PAIRS),
-                in_=bank[:].rearrange("p u c h r -> p (c h r) u"),
-            )
+            out = y_grouped[:, rt, :].bitcast(F32).rearrange("p (s u) -> p s u", u=PAIRS)
+            in_ = bank[:].rearrange("p u c h r -> p (c h r) u")
+            if rt in GROUPED_ON_VECTOR:
+                nc.vector.tensor_copy(out=out, in_=in_)
+            else:
+                nc.scalar.copy(out=out, in_=in_)
 
         def quantise(rt):
             nc.vector.quantize_mx(
@@ -169,40 +179,71 @@ def tile_transposedattentiontransformer_pb_kernel(
                         start=(c == 0),
                         stop=(c == PASSES - 1),
                     )
-                nc.vector.tensor_tensor(out=result[:, rt, cols], in0=bank[:], in1=result[:, rt, cols], op=ADD)
-                nc.sync.dma_start(out=out_rows[rt * P : (rt + 1) * P, cols], in_=result[:, rt, cols])
+                pieces = 2 if rt == ROW_TILES - 1 and half == HALVES - 1 else 1
+                width = HALF // pieces
+                for piece in range(pieces):
+                    here = slice(half * HALF + piece * width, half * HALF + (piece + 1) * width)
+                    nc.vector.tensor_tensor(
+                        out=result[:, rt, here],
+                        in0=bank[:, piece * width : (piece + 1) * width],
+                        in1=result[:, rt, here],
+                        op=ADD,
+                    )
+                    nc.sync.dma_start(out=out_rows[rt * P : (rt + 1) * P, here], in_=result[:, rt, here])
 
-        for half in range(HALVES):
-            bank = banks.tile([P, HALF], F32, tag="bank")
-            for j in range(SLABS_PER_PASS):
-                s = half * SLABS_PER_PASS + j
-                nc.tensor.matmul(
-                    out=bank[:, j * P : (j + 1) * P],
-                    lhsT=ident_bf16[:, s : s + 1].to_broadcast([P, P]),
-                    rhs=bias_slabs[:],
-                    start=True,
-                    stop=True,
-                )
-            nc.scalar.copy(out=bias_all[:, half * HALF : (half + 1) * HALF], in_=bank[:])
-        flip_attn(0)
+        def spread_bias():
+            for half in range(HALVES):
+                bank = banks.tile([P, HALF], F32, tag="bank")
+                for j in range(SLABS_PER_PASS):
+                    s = half * SLABS_PER_PASS + j
+                    nc.tensor.matmul(
+                        out=bank[:, j * P : (j + 1) * P],
+                        lhsT=ident_bf16[:, s : s + 1].to_broadcast([P, P]),
+                        rhs=bias_slabs[:],
+                        start=True,
+                        stop=True,
+                    )
+                nc.scalar.copy(out=bias_all[:, half * HALF : (half + 1) * HALF], in_=bank[:])
 
         def add_bias(rt):
-            nc.vector.tensor_tensor(out=result[:, rt, :], in0=shortcut_sb[:, rt, :], in1=bias_all[:], op=ADD)
+            if rt < ADDED_ON_GPSIMD:
+                nc.vector.tensor_tensor(out=result[:, rt, :], in0=shortcut_sb[:, rt, :], in1=bias_all[:], op=ADD)
+            else:
+                for half in range(HALVES):
+                    cols = slice(half * HALF, (half + 1) * HALF)
+                    nc.gpsimd.tensor_tensor(
+                        out=result[:, rt, cols], in0=shortcut_sb[:, rt, cols], in1=bias_all[:, cols], op=ADD
+                    )
+
+        bank = banks.tile([P, HALF], F32, tag="bank")
+        for i in range(WARM_UP):
+            nc.tensor.matmul(out=bank[:], lhsT=warm_sb[:, 0:P], rhs=warm_sb[:], start=True, stop=True)
 
         def is_tile(rt):
             return 0 <= rt < ROW_TILES
 
-        for step in range(ROW_TILES + MX_LAG):
+        flip_attn(0)
+        for step in range(ROW_TILES + 2):
             if is_tile(step):
                 flip_v(step)
-            if is_tile(step - 2):
-                flip_y(step - 2)
-            if step == 3:
+            if step == 0:
+                spread_bias()
+            if step == 1:
                 flip_attn(1)
+            if step < ROW_TILES:
+                if is_tile(step - 1):
+                    attend(step - 1)
+                if is_tile(step - 2):
+                    flip_y(step - 2)
+            else:
+                flip_y(step - 2)
+                if is_tile(step - 1):
+                    attend(step - 1)
             if is_tile(step - 1):
-                attend(step - 1)
+                add_bias(step - 1)
             if is_tile(step - 2):
-                add_bias(step - 2)
                 quantise(step - 2)
-            if is_tile(step - MX_LAG):
-                project(step - MX_LAG)
+            if step in PROJECT_AFTER:
+                first = 2 * PROJECT_AFTER.index(step)
+                project(first)
+                project(first + 1)

@@ -100,7 +100,7 @@ def tile_transposedattentiontransformer_pb_kernel(
         load_v(2)
         for rt in range(3, ROW_TILES):
             load_shortcut(rt - 3)
-            if rt == 4:
+            if rt == 6:
                 load_w()
             load_v(rt)
         for rt in range(ROW_TILES - 3, ROW_TILES):

@@ -27,8 +27,7 @@ HALVES = 2
 PAIRS = 2
 
 PROJECT_AFTER = (5, 7, 8, 9)
-GROUPED_ON_VECTOR = (0, 2, 4)
-ADDED_ON_GPSIMD = 5
+ADDED_ON_GPSIMD = 7
 
 WARM_UP = 4
 
@@ -153,12 +152,10 @@ def tile_transposedattentiontransformer_pb_kernel(
                     nc.tensor.transpose(
                         bank[:, u, :, h, :], y_sb[:, rt, first : first + 2 * P].bitcast(F32), ident_f32[:]
                     )
-            out = y_grouped[:, rt, :].bitcast(F32).rearrange("p (s u) -> p s u", u=PAIRS)
-            in_ = bank[:].rearrange("p u c h r -> p (c h r) u")
-            if rt in GROUPED_ON_VECTOR:
-                nc.vector.tensor_copy(out=out, in_=in_)
-            else:
-                nc.scalar.copy(out=out, in_=in_)
+            nc.scalar.copy(
+                out=y_grouped[:, rt, :].bitcast(F32).rearrange("p (s u) -> p s u", u=PAIRS),
+                in_=bank[:].rearrange("p u c h r -> p (c h r) u"),
+            )
 
         def quantise(rt):
             nc.vector.quantize_mx(
@@ -203,7 +200,7 @@ def tile_transposedattentiontransformer_pb_kernel(
                         start=True,
                         stop=True,
                     )
-                nc.scalar.copy(out=bias_all[:, half * HALF : (half + 1) * HALF], in_=bank[:])
+                nc.vector.tensor_copy(out=bias_all[:, half * HALF : (half + 1) * HALF], in_=bank[:])
 
         def add_bias(rt):
             if rt < ADDED_ON_GPSIMD:
@@ -228,7 +225,7 @@ def tile_transposedattentiontransformer_pb_kernel(
                 flip_v(step)
             if step == 0:
                 spread_bias()
-            if step == 1:
+            if step == 2:
                 flip_attn(1)
             if step < ROW_TILES:
                 if is_tile(step - 1):

from contextlib import ExitStack

import concourse.mybir as mybir
from concourse.masks import make_identity

BF16 = mybir.dt.bfloat16
F32 = mybir.dt.float32
I32 = mybir.dt.int32
U8 = mybir.dt.uint8
U32 = mybir.dt.uint32
FP8X4 = mybir.dt.float8_e4m3fn_x4
FP4X4 = mybir.dt.float4_e2m1fn_x4
ADD = mybir.AluOpType.add

P = 128
WIDTH = 1024
ROW_TILES = 8
BATCHES = 2
SLABS = 8
PASSES = 2
SLABS_PER_PASS = 4
HEADS_PER_TILE = 2
HEAD_ROWS = 64
HEADS = 8
HALF = 512
HALVES = 2
PAIRS = 2

PROJECT_AFTER = (5, 7, 8, 9)
ADDED_ON_GPSIMD = 7

WARM_UP = 4

FLOPS = 2 * 1024 * 1024 * 1024 + 2 * 16 * 128 * 128 * 512


def tile_transposedattentiontransformer_pb_kernel(
    tc, attn, v, w_proj_words, w_proj_scales, b_proj, shortcut, out
):
    nc = tc.nc
    v_rows = v.rearrange("b g (r s) e -> (b g r) (s e)", s=SLABS)
    attn_rows = attn.rearrange("b g (a x) e -> b (g a) (x e)", x=SLABS)
    shortcut_rows = shortcut.flatten_outer_dims()
    out_rows = out.flatten_outer_dims()

    with ExitStack() as ctx:
        keep = ctx.enter_context(tc.tile_pool(name="keep", bufs=1))
        banks = ctx.enter_context(tc.psum_pool(name="banks", bufs=8))
        ctx.enter_context(tc.manual_schedule())

        ident_bf16 = keep.tile([P, P], BF16)
        ident_f32 = keep.tile([P, P], F32)
        bias_slabs = keep.tile([P, P], BF16)
        bias_all = keep.tile([P, WIDTH], BF16)
        attn_sb = keep.tile([P, BATCHES, WIDTH], BF16)
        attn_t = keep.tile([P, BATCHES, WIDTH], BF16)
        v_sb = keep.tile([P, ROW_TILES, WIDTH], BF16)
        v_t = keep.tile([P, ROW_TILES, WIDTH], BF16)
        y_sb = keep.tile([P, ROW_TILES, WIDTH], BF16)
        y_grouped = keep.tile([P, ROW_TILES, WIDTH], BF16, align_bytes=64)
        y_codes = keep.tile([P, ROW_TILES, PASSES * P], U32, align_bytes=64)
        y_scales = keep.tile([P, ROW_TILES, PASSES * P], U8, align_bytes=64)
        w_words = keep.tile([P, PASSES, 2 * WIDTH], U8, align_bytes=64)
        w_scales = keep.tile([P, PASSES, WIDTH], U8, align_bytes=64)
        shortcut_sb = keep.tile([P, ROW_TILES, WIDTH], BF16)
        result = keep.tile([P, ROW_TILES, WIDTH], F32)

        warm_sb = keep.tile([P, HALF], BF16)
        nc.vector.memset(warm_sb[:].bitcast(F32), 0.0)
        nc.gpsimd.memset(bias_slabs[:], 0.0)
        make_identity(nc, ident_bf16[:])
        make_identity(nc, ident_f32[:])
        nc.vector.memset(w_scales[:].bitcast(I32), 0)

        def load_attn(b):
            nc.sync.dma_start(out=attn_sb[:, b, :], in_=attn_rows[b])

        def load_v(rt):
            nc.sync.dma_start(out=v_sb[:, rt, :], in_=v_rows[rt * P : (rt + 1) * P, :])

        def load_shortcut(rt):
            nc.sync.dma_start(out=shortcut_sb[:, rt, :], in_=shortcut_rows[rt * P : (rt + 1) * P, :])

        def load_w():
            nc.sync.dma_start(
                out=w_words[:].bitcast(I32), in_=w_proj_words.bitcast(I32).rearrange("c p n -> p c n")
            )
            for quadrant in range(4):
                nc.sync.dma_start(
                    out=w_scales[32 * quadrant : 32 * quadrant + 4, :, :].bitcast(I32),
                    in_=w_proj_scales.bitcast(I32)[:, 4 * quadrant : 4 * quadrant + 4, :].rearrange("c i n -> i c n"),
                )

        load_attn(0)
        load_v(0)
        nc.sync.dma_start(out=bias_slabs[0:SLABS, :], in_=b_proj.rearrange("(s n) -> s n", n=P))
        load_v(1)
        load_attn(1)
        load_v(2)
        for rt in range(3, ROW_TILES):
            load_shortcut(rt - 3)
            if rt == 6:
                load_w()
            load_v(rt)
        for rt in range(ROW_TILES - 3, ROW_TILES):
            load_shortcut(rt)

        def flip_attn(b):
            bank = banks.tile([P, SLABS, P], BF16, tag="bank")
            for x in range(SLABS):
                nc.tensor.transpose(bank[:, x, :], attn_sb[:, b, x * P : (x + 1) * P], ident_bf16[:])
            nc.vector.tensor_copy(
                out=attn_t[:, b, :].rearrange("e (a x) -> e a x", x=SLABS),
                in_=bank[:].rearrange("e x a -> e a x"),
            )

        def flip_v(rt):
            bank = banks.tile([P, HEADS_PER_TILE, SLABS_PER_PASS, PASSES, HEAD_ROWS], BF16, tag="bank")
            for slab in range(SLABS):
                c, j = divmod(slab, SLABS_PER_PASS)
                nc.tensor.transpose(bank[:, :, j, c, :], v_sb[:, rt, slab * P : (slab + 1) * P], ident_bf16[:])
            nc.scalar.copy(
                out=v_t[:, rt, :].bitcast(F32), in_=bank[:].rearrange("e h j c r -> e (h j c r)").bitcast(F32)
            )

        def attend(rt):
            bank = banks.tile([P, HEADS_PER_TILE, HALF], BF16, tag="bank")
            for h in range(HEADS_PER_TILE):
                b, g = divmod(rt * HEADS_PER_TILE + h, HEADS)
                for j in range(SLABS_PER_PASS):
                    first = (h * SLABS_PER_PASS + j) * P
                    nc.tensor.matmul(
                        out=bank[:, h, j * P : (j + 1) * P],
                        lhsT=v_t[:, rt, first : first + P],
                        rhs=attn_t[:, b, g * P : (g + 1) * P],
                        start=True,
                        stop=True,
                    )
            nc.scalar.copy(
                out=y_sb[:, rt, :].bitcast(F32).rearrange("m (h u p) -> m h u p", h=HEADS_PER_TILE, u=PAIRS),
                in_=bank[:]
                .rearrange("m h k -> m (h k)")
                .bitcast(F32)
                .rearrange("m (h p u) -> m h u p", h=HEADS_PER_TILE, u=PAIRS),
            )

        def flip_y(rt):
            bank = banks.tile([P, PAIRS, PASSES, HEADS_PER_TILE, HEAD_ROWS], F32, tag="bank")
            for h in range(HEADS_PER_TILE):
                for u in range(PAIRS):
                    first = (h * PAIRS + u) * 2 * P
                    nc.tensor.transpose(
                        bank[:, u, :, h, :], y_sb[:, rt, first : first + 2 * P].bitcast(F32), ident_f32[:]
                    )
            nc.scalar.copy(
                out=y_grouped[:, rt, :].bitcast(F32).rearrange("p (s u) -> p s u", u=PAIRS),
                in_=bank[:].rearrange("p u c h r -> p (c h r) u"),
            )

        def quantise(rt):
            nc.vector.quantize_mx(
                out=y_codes[:, rt, :].bitcast(FP8X4), scales=y_scales[:, rt, :], in_=y_grouped[:, rt, :]
            )

        def project(rt):
            for half in range(HALVES):
                cols = slice(half * HALF, (half + 1) * HALF)
                bank = banks.tile([P, HALF], F32, tag="bank")
                for c in range(PASSES):
                    nc.tensor.matmul_mx(
                        out=bank[:],
                        lhsT=y_codes[:, rt, c * P : (c + 1) * P].bitcast(FP8X4),
                        lhsT_scale=y_scales[:, rt, c * P : (c + 1) * P],
                        rhs=w_words[:, c, 2 * half * HALF : 2 * (half + 1) * HALF].bitcast(FP4X4),
                        rhs_scale=w_scales[:, c, cols],
                        start=(c == 0),
                        stop=(c == PASSES - 1),
                    )
                pieces = 2 if rt == ROW_TILES - 1 and half == HALVES - 1 else 1
                width = HALF // pieces
                for piece in range(pieces):
                    here = slice(half * HALF + piece * width, half * HALF + (piece + 1) * width)
                    nc.vector.tensor_tensor(
                        out=result[:, rt, here],
                        in0=bank[:, piece * width : (piece + 1) * width],
                        in1=result[:, rt, here],
                        op=ADD,
                    )
                    nc.sync.dma_start(out=out_rows[rt * P : (rt + 1) * P, here], in_=result[:, rt, here])

        def spread_bias():
            for half in range(HALVES):
                bank = banks.tile([P, HALF], F32, tag="bank")
                for j in range(SLABS_PER_PASS):
                    s = half * SLABS_PER_PASS + j
                    nc.tensor.matmul(
                        out=bank[:, j * P : (j + 1) * P],
                        lhsT=ident_bf16[:, s : s + 1].to_broadcast([P, P]),
                        rhs=bias_slabs[:],
                        start=True,
                        stop=True,
                    )
                nc.vector.tensor_copy(out=bias_all[:, half * HALF : (half + 1) * HALF], in_=bank[:])

        def add_bias(rt):
            if rt < ADDED_ON_GPSIMD:
                nc.vector.tensor_tensor(out=result[:, rt, :], in0=shortcut_sb[:, rt, :], in1=bias_all[:], op=ADD)
            else:
                for half in range(HALVES):
                    cols = slice(half * HALF, (half + 1) * HALF)
                    nc.gpsimd.tensor_tensor(
                        out=result[:, rt, cols], in0=shortcut_sb[:, rt, cols], in1=bias_all[:, cols], op=ADD
                    )

        bank = banks.tile([P, HALF], F32, tag="bank")
        for i in range(WARM_UP):
            nc.tensor.matmul(out=bank[:], lhsT=warm_sb[:, 0:P], rhs=warm_sb[:], start=True, stop=True)

        def is_tile(rt):
            return 0 <= rt < ROW_TILES

        flip_attn(0)
        for step in range(ROW_TILES + 2):
            if is_tile(step):
                flip_v(step)
            if step == 0:
                spread_bias()
            if step == 2:
                flip_attn(1)
            if step < ROW_TILES:
                if is_tile(step - 1):
                    attend(step - 1)
                if is_tile(step - 2):
                    flip_y(step - 2)
            else:
                flip_y(step - 2)
                if is_tile(step - 1):
                    attend(step - 1)
            if is_tile(step - 1):
                add_bias(step - 1)
            if is_tile(step - 2):
                quantise(step - 2)
            if step in PROJECT_AFTER:
                first = 2 * PROJECT_AFTER.index(step)
                project(first)
                project(first + 1)
